import numpy as np
import ml_dtypes


def mxq(x, axis, fmt="e4m3"):
    dtype, down = {"e4m3": (ml_dtypes.float8_e4m3fn, 7), "e5m2": (ml_dtypes.float8_e5m2, 14)}[fmt]
    v = np.moveaxis(np.asarray(x, np.float32).astype(ml_dtypes.bfloat16).astype(np.float64), axis, -1)
    blocks = v.reshape(v.shape[:-1] + (-1, 32))
    amax = np.abs(blocks).max(-1, keepdims=True)
    byte = np.maximum(np.where(amax > 0, np.frexp(amax)[1] - 1 + 127, 0) - down, 1)
    scale = np.exp2(byte - 127.0)
    codes = (blocks / scale).astype(np.float32).astype(dtype).astype(np.float64)
    return np.moveaxis((codes * scale).reshape(v.shape), -1, axis)


WIDE = False


def mx_kscale(k):
    if not WIDE:
        return np.ones(k)
    levels = np.array([10, -10, 5, -5, 0])
    a = np.random.permutation(np.resize(levels, k // 512 * 4)).reshape(k // 512, 4)
    idx = np.arange(k)
    return np.exp2(a[idx // 512, idx % 128 // 32])


BF16 = ml_dtypes.bfloat16


def bf(x):
    return np.asarray(x, np.float32).astype(BF16)


def f64(x):
    return np.asarray(x).astype(np.float64)


B, K, N = 4096, 512, 1024


def setup_inputs():
    s = mx_kscale(K)
    return {"x": bf(np.random.standard_normal((B, K)) * s),
            "dft_real": bf(np.random.standard_normal((N, K)) / np.sqrt(K) / s[None, :]),
            "dft_imag": bf(np.random.standard_normal((N, K)) / np.sqrt(K) / s[None, :])}


def reference(x, dft_real, dft_imag):
    xq = mxq(f64(x), 1, "e4m3")
    rxs = xq @ mxq(f64(dft_real), 1, "e4m3").T
    ixs = xq @ mxq(f64(dft_imag), 1, "e4m3").T
    mag = np.log(rxs * rxs + ixs * ixs)
    return mag

@@ -1,0 +1,229 @@
+from contextlib import ExitStack
+
+import concourse.mybir as mybir
+from concourse.masks import make_identity
+
+F32 = mybir.dt.float32
+BF16 = mybir.dt.bfloat16
+U32 = mybir.dt.uint32
+U8 = mybir.dt.uint8
+FP8X4 = mybir.dt.float8_e4m3fn_x4
+FUNC = mybir.ActivationFunctionType
+ALU = mybir.AluOpType
+AXIS = mybir.AxisListType
+
+B, K, N = 4096, 512, 1024
+FLOPS = 2 * B * K * 2 * N
+P = 128
+HALF = 512
+GROUPS = 8
+MANUAL = True
+ACT_I = (0, 4, 5, 9, 15, 24, 34, 42, 49, 54)
+LAG_G2 = 6
+LAG_G1 = 4
+LAG_V = 1
+X_T, X_X, X_Q = 1, 3, 5
+G1_PAIRS = (0, 1,)
+VU_PAIRS = (14, 15,)
+
+
+def tile_dft_t_kernel(tc, x, dft_real, dft_imag, out):
+    nc = tc.nc
+    with ExitStack() as ctx:
+        if MANUAL:
+            ctx.enter_context(tc.manual_schedule())
+        const = ctx.enter_context(tc.tile_pool(name="const", bufs=1))
+        raw = ctx.enter_context(tc.tile_pool(name="raw", bufs=1))
+        keep = ctx.enter_context(tc.tile_pool(name="keep", bufs=1))
+        stage = ctx.enter_context(tc.tile_pool(name="stage", bufs=3))
+        work = ctx.enter_context(tc.tile_pool(name="work", bufs=1))
+        psum = ctx.enter_context(tc.psum_pool(name="psum", bufs=1))
+
+        raws = {}
+
+        def load_x(g):
+            t = raw.tile([P, 4 * K], BF16, name="rawx%d" % g)
+            nc.sync.dma_start(
+                out=t[:].rearrange("p (t k) -> p t k", t=4),
+                in_=x[512 * g : 512 * (g + 1), :].rearrange("(p t) k -> p t k", t=4),
+            )
+            raws["x%d" % g] = t
+
+        def load_w(m, h):
+            src = (dft_real, dft_imag)[m]
+            t = raw.tile([P, 4 * K], BF16, name="raww%d%d" % (m, h))
+            nc.sync.dma_start(
+                out=t[:].rearrange("p (t k) -> p t k", t=4),
+                in_=src[HALF * h : HALF * (h + 1), :].rearrange("(t p) k -> p t k", p=P),
+            )
+            raws["w%d%d" % (m, h)] = t
+
+        load_x(0)
+        load_w(0, 0)
+        load_w(1, 0)
+        load_w(0, 1)
+        load_w(1, 1)
+        for g in range(1, GROUPS):
+            load_x(g)
+
+        ident = const.tile([P, P], F32, name="ident")
+        make_identity(nc, ident[:])
+        warm = const.tile([P, 1], F32, name="warm")
+        nc.vector.memset(warm[:], 1.0)
+        warm2 = const.tile([P, 1], F32, name="warm2")
+        nc.scalar.activation(out=warm2[:], in_=warm[:], func=FUNC.Ln)
+
+        tbanks = {}
+        grouped_of = {}
+        quantised = {}
+
+        def transposes(name, tags):
+            words = raws[name][:].bitcast(F32)
+            pair = []
+            for half in range(2):
+                bank = psum.tile([P, 2, 2, P], F32, tag=tags[half], name="t%d%s" % (half, name),
+                                 bufs=(2 if tags[half] == "tp" else 3))
+                for bb in range(2):
+                    for u in range(2):
+                        c0 = 256 * (2 * half + bb) + 128 * u
+                        nc.tensor.transpose(bank[:, bb, u, :], words[:, c0 : c0 + 128], ident[:])
+                pair.append(bank)
+            tbanks[name] = pair
+
+        def exits(name, engines):
+            grouped = stage.tile([P, 4 * HALF], BF16, tag="grouped", name="g" + name, align_bytes=64)
+            gw = grouped[:].bitcast(F32).rearrange("p (b c u) -> p b c u", b=4, u=2)
+            for half in range(2):
+                src_view = tbanks[name][half][:].rearrange("p b u c -> p b c u")
+                dst_view = gw[:, 2 * half : 2 * half + 2]
+                if engines[half] == "a":
+                    nc.scalar.copy(out=dst_view, in_=src_view)
+                else:
+                    nc.vector.tensor_copy(out=dst_view, in_=src_view)
+            grouped_of[name] = grouped
+
+        def quantise(name):
+            codes = keep.tile([P, HALF], U32, name="c" + name, align_bytes=64)
+            scales = keep.tile([P, HALF], U8, name="s" + name, align_bytes=64)
+            nc.vector.quantize_mx(out=codes[:].bitcast(FP8X4), scales=scales[:], in_=grouped_of[name][:])
+            quantised[name] = (codes, scales)
+
+        units = [(0, t, 0) for t in range(4)] + [(0, t, 1) for t in range(4)]
+        for g in range(1, GROUPS):
+            units += [(g, t, h) for t in range(4) for h in range(2)]
+        n_units = len(units)
+
+        banks = {}
+
+        def mm(s):
+            g, t, h = units[s]
+            xc, xs = quantised["x%d" % g]
+            pair = []
+            for m in range(2):
+                wc, ws = quantised["w%d%d" % (m, h)]
+                acc = psum.tile([P, HALF], F32, tag=("r", "i")[m], name="acc%d_%d" % (m, s), bufs=3)
+                nc.tensor.matmul_mx(
+                    out=acc[:],
+                    lhsT=xc[:, P * t : P * (t + 1)].bitcast(FP8X4),
+                    lhsT_scale=xs[:, P * t : P * (t + 1)],
+                    rhs=wc[:].bitcast(FP8X4),
+                    rhs_scale=ws[:],
+                    start=True,
+                    stop=True,
+                )
+                pair.append(acc)
+            banks[s] = pair
+
+        sq = {}
+        count = {}
+        pending = []
+        served = [0]
+
+        def squares(s):
+            g, t, h = units[s]
+            pk = 2 * g + t // 2
+            if pk not in sq:
+                a_t = work.tile([P, 2 * N], F32, tag="a", name="a%d" % pk, bufs=6)
+                b_t = work.tile([P, 2 * N], F32, tag="b", name="b%d" % pk, bufs=4)
+                sq[pk] = (a_t, b_t)
+                count[pk] = [0, 0]
+            a_t, b_t = sq[pk]
+            tt = t % 2
+            c0 = N * tt + HALF * h
+            acc_r, acc_i = banks[s]
+            nc.scalar.activation(out=a_t[:, c0 : c0 + HALF], in_=acc_r[:], func=FUNC.Square)
+            if s in ACT_I:
+                nc.scalar.activation(out=b_t[:, c0 : c0 + HALF], in_=acc_i[:], func=FUNC.Square)
+            else:
+                nc.vector.tensor_reduce(
+                    out=b_t[:, c0 : c0 + HALF],
+                    in_=acc_i[:].unsqueeze(2).to_broadcast([P, HALF, 2]),
+                    axis=AXIS.X,
+                    op=ALU.mult,
+                )
+            count[pk][tt] += 1
+            if pk in VU_PAIRS:
+                cols = slice(c0, c0 + HALF)
+                nc.vector.tensor_tensor(out=a_t[:, cols], in0=a_t[:, cols], in1=b_t[:, cols], op=ALU.add)
+                pending.append((s + LAG_V, pk, c0, HALF))
+            elif pk in G1_PAIRS:
+                if count[pk][tt] == 2:
+                    cols = slice(N * tt, N * (tt + 1))
+                    nc.gpsimd.tensor_tensor(out=a_t[:, cols], in0=a_t[:, cols], in1=b_t[:, cols], op=ALU.add)
+                    pending.append((s + LAG_G1, pk, N * tt, N))
+            elif count[pk][0] + count[pk][1] == 4:
+                nc.gpsimd.tensor_tensor(out=a_t[:], in0=a_t[:], in1=b_t[:], op=ALU.add)
+                pending.append((s + LAG_G2, pk, 0, N))
+                pending.append((s + LAG_G2 + 2, pk, N, N))
+
+        def finish(pk, c0, width):
+            a_t = sq[pk][0]
+            part = a_t[:, c0 : c0 + width]
+            nc.scalar.activation(out=part, in_=part, func=FUNC.Ln)
+            g = pk // 2
+            t = 2 * (pk % 2) + c0 // N
+            n0 = c0 % N
+            dst = out[512 * g : 512 * (g + 1), :].rearrange("(p t) n -> p t n", t=4)
+            nc.sync.dma_start(out=dst[:, t, n0 : n0 + width], in_=part)
+
+        def finish_due(s):
+            pending[served[0] :] = sorted(pending[served[0] :])
+            while served[0] < len(pending) and pending[served[0]][0] <= s:
+                item = pending[served[0]]
+                served[0] += 1
+                finish(item[1], item[2], item[3])
+
+        transposes("x0", ("tp", "tp"))
+        transposes("w00", ("i", "i"))
+        exits("x0", "va")
+        transposes("w10", ("tp", "tp"))
+        quantise("x0")
+        exits("w00", "av")
+        quantise("w00")
+        transposes("w01", ("i", "r"))
+        exits("w10", "av")
+        quantise("w10")
+        mm(0)
+        mm(1)
+        for s in range(n_units):
+            if s == 1:
+                transposes("w11", ("tp", "tp"))
+            if s == 2:
+                quantise("w11")
+            g = s // 8 + 1
+            if g < GROUPS and s % 8 == X_T:
+                transposes("x%d" % g, ("tp", "tp"))
+            if g < GROUPS and s % 8 == X_Q:
+                quantise("x%d" % g)
+            if s + 2 < n_units:
+                mm(s + 2)
+            squares(s)
+            if s == 0:
+                exits("w01", "av")
+            if s == 1:
+                quantise("w01")
+                exits("w11", "av")
+            if g < GROUPS and s % 8 == X_X:
+                exits("x%d" % g, "vv")
+            finish_due(s)
+        finish_due(10 * n_units)

@@ -10,7 +10,6 @@ U8 = mybir.dt.uint8
 FP8X4 = mybir.dt.float8_e4m3fn_x4
 FUNC = mybir.ActivationFunctionType
 ALU = mybir.AluOpType
-AXIS = mybir.AxisListType
 
 B, K, N = 4096, 512, 1024
 FLOPS = 2 * B * K * 2 * N
@@ -18,7 +17,7 @@ P = 128
 HALF = 512
 GROUPS = 8
 MANUAL = True
-ACT_I = (0, 4, 5, 9, 15, 24, 34, 42, 49, 54)
+ACT_I = (1, 3, 4, 5, 7, 11, 19, 23, 28, 35, 43, 51, 57)
 LAG_G2 = 6
 LAG_G1 = 4
 LAG_V = 1
@@ -134,6 +133,15 @@ def tile_dft_t_kernel(tc, x, dft_real, dft_imag, out):
                 pair.append(acc)
             banks[s] = pair
 
+        copies = {}
+
+        def copy_i(s):
+            if s >= n_units or s in ACT_I:
+                return
+            c_t = work.tile([P, HALF], F32, tag="c", name="c%d" % s, bufs=4)
+            nc.vector.tensor_copy(out=c_t[:], in_=banks[s][1][:])
+            copies[s] = c_t
+
         sq = {}
         count = {}
         pending = []
@@ -155,12 +163,7 @@ def tile_dft_t_kernel(tc, x, dft_real, dft_imag, out):
             if s in ACT_I:
                 nc.scalar.activation(out=b_t[:, c0 : c0 + HALF], in_=acc_i[:], func=FUNC.Square)
             else:
-                nc.vector.tensor_reduce(
-                    out=b_t[:, c0 : c0 + HALF],
-                    in_=acc_i[:].unsqueeze(2).to_broadcast([P, HALF, 2]),
-                    axis=AXIS.X,
-                    op=ALU.mult,
-                )
+                nc.vector.tensor_tensor(out=b_t[:, c0 : c0 + HALF], in0=acc_i[:], in1=copies[s][:], op=ALU.mult)
             count[pk][tt] += 1
             if pk in VU_PAIRS:
                 cols = slice(c0, c0 + HALF)
@@ -205,6 +208,8 @@ def tile_dft_t_kernel(tc, x, dft_real, dft_imag, out):
         quantise("w10")
         mm(0)
         mm(1)
+        copy_i(0)
+        copy_i(1)
         for s in range(n_units):
             if s == 1:
                 transposes("w11", ("tp", "tp"))
@@ -218,6 +223,7 @@ def tile_dft_t_kernel(tc, x, dft_real, dft_imag, out):
             if s + 2 < n_units:
                 mm(s + 2)
             squares(s)
+            copy_i(s + 2)
             if s == 0:
                 exits("w01", "av")
             if s == 1:

@@ -24,6 +24,7 @@ LAG_V = 1
 X_T, X_X, X_Q = 1, 3, 5
 G1_PAIRS = (0, 1,)
 VU_PAIRS = (14, 15,)
+V1_PAIRS = ()
 
 
 def tile_dft_t_kernel(tc, x, dft_real, dft_imag, out):
@@ -151,8 +152,8 @@ def tile_dft_t_kernel(tc, x, dft_real, dft_imag, out):
             g, t, h = units[s]
             pk = 2 * g + t // 2
             if pk not in sq:
-                a_t = work.tile([P, 2 * N], F32, tag="a", name="a%d" % pk, bufs=6)
-                b_t = work.tile([P, 2 * N], F32, tag="b", name="b%d" % pk, bufs=4)
+                a_t = work.tile([P, 2 * N], F32, tag="a", name="a%d" % pk, bufs=5)
+                b_t = work.tile([P, 2 * N], F32, tag="b", name="b%d" % pk, bufs=6)
                 sq[pk] = (a_t, b_t)
                 count[pk] = [0, 0]
             a_t, b_t = sq[pk]
@@ -169,6 +170,11 @@ def tile_dft_t_kernel(tc, x, dft_real, dft_imag, out):
                 cols = slice(c0, c0 + HALF)
                 nc.vector.tensor_tensor(out=a_t[:, cols], in0=a_t[:, cols], in1=b_t[:, cols], op=ALU.add)
                 pending.append((s + LAG_V, pk, c0, HALF))
+            elif pk in V1_PAIRS:
+                if count[pk][tt] == 2:
+                    cols = slice(N * tt, N * (tt + 1))
+                    nc.vector.tensor_tensor(out=a_t[:, cols], in0=a_t[:, cols], in1=b_t[:, cols], op=ALU.add)
+                    pending.append((s + LAG_V, pk, N * tt, N))
             elif pk in G1_PAIRS:
                 if count[pk][tt] == 2:
                     cols = slice(N * tt, N * (tt + 1))
@@ -180,9 +186,9 @@ def tile_dft_t_kernel(tc, x, dft_real, dft_imag, out):
                 pending.append((s + LAG_G2 + 2, pk, N, N))
 
         def finish(pk, c0, width):
-            a_t = sq[pk][0]
-            part = a_t[:, c0 : c0 + width]
-            nc.scalar.activation(out=part, in_=part, func=FUNC.Ln)
+            a_t, b_t = sq[pk]
+            part = b_t[:, c0 : c0 + width]
+            nc.scalar.activation(out=part, in_=a_t[:, c0 : c0 + width], func=FUNC.Ln)
             g = pk // 2
             t = 2 * (pk % 2) + c0 // N
             n0 = c0 % N

@@ -10,28 +10,24 @@ U8 = mybir.dt.uint8
 FP8X4 = mybir.dt.float8_e4m3fn_x4
 FUNC = mybir.ActivationFunctionType
 ALU = mybir.AluOpType
+AXIS = mybir.AxisListType
 
 B, K, N = 4096, 512, 1024
 FLOPS = 2 * B * K * 2 * N
 P = 128
 HALF = 512
 GROUPS = 8
-MANUAL = True
-ACT_I = (1, 3, 4, 5, 7, 11, 19, 23, 28, 35, 43, 51, 57)
-LAG_G2 = 6
-LAG_G1 = 4
-LAG_V = 1
-X_T, X_X, X_Q = 1, 3, 5
-G1_PAIRS = (0, 1,)
-VU_PAIRS = (14, 15,)
-V1_PAIRS = ()
+ACT_I = (0, 1, 2, 4, 5, 11, 19, 27, 35, 39, 43, 51)
+LAG = {4: 6, 2: 4, 1: 4}
+X_T, X_X, X_Q = 0, 1, 3
+FIRST = (2, 3, 4)
+UNITS_PER_ADD = {0: 1, 1: 1, 14: 2, 15: 1}
 
 
 def tile_dft_t_kernel(tc, x, dft_real, dft_imag, out):
     nc = tc.nc
     with ExitStack() as ctx:
-        if MANUAL:
-            ctx.enter_context(tc.manual_schedule())
+        ctx.enter_context(tc.manual_schedule())
         const = ctx.enter_context(tc.tile_pool(name="const", bufs=1))
         raw = ctx.enter_context(tc.tile_pool(name="raw", bufs=1))
         keep = ctx.enter_context(tc.tile_pool(name="keep", bufs=1))
@@ -113,6 +109,16 @@ def tile_dft_t_kernel(tc, x, dft_real, dft_imag, out):
             units += [(g, t, h) for t in range(4) for h in range(2)]
         n_units = len(units)
 
+        at_t = {}
+        at_x = {}
+        at_q = {}
+        for g in range(1, GROUPS):
+            base = 8 * (g - 1)
+            steps = FIRST if g == 1 else (base + X_T, base + X_X, base + X_Q)
+            at_t[steps[0]] = g
+            at_x[steps[1]] = g
+            at_q[steps[2]] = g
+
         banks = {}
 
         def mm(s):
@@ -134,61 +140,63 @@ def tile_dft_t_kernel(tc, x, dft_real, dft_imag, out):
                 pair.append(acc)
             banks[s] = pair
 
-        copies = {}
-
-        def copy_i(s):
-            if s >= n_units or s in ACT_I:
-                return
-            c_t = work.tile([P, HALF], F32, tag="c", name="c%d" % s, bufs=4)
-            nc.vector.tensor_copy(out=c_t[:], in_=banks[s][1][:])
-            copies[s] = c_t
-
         sq = {}
-        count = {}
+        ready = {}
         pending = []
         served = [0]
 
-        def squares(s):
+        def place(s):
             g, t, h = units[s]
-            pk = 2 * g + t // 2
+            return 2 * g + t // 2, N * (t % 2) + HALF * h
+
+        def squares_scalar(s):
+            pk, c0 = place(s)
             if pk not in sq:
-                a_t = work.tile([P, 2 * N], F32, tag="a", name="a%d" % pk, bufs=5)
-                b_t = work.tile([P, 2 * N], F32, tag="b", name="b%d" % pk, bufs=6)
+                a_t = work.tile([P, 2 * N], F32, tag="a", name="a%d" % pk, bufs=6)
+                b_t = work.tile([P, 2 * N], F32, tag="b", name="b%d" % pk, bufs=4)
                 sq[pk] = (a_t, b_t)
-                count[pk] = [0, 0]
+                ready[pk] = []
             a_t, b_t = sq[pk]
-            tt = t % 2
-            c0 = N * tt + HALF * h
-            acc_r, acc_i = banks[s]
-            nc.scalar.activation(out=a_t[:, c0 : c0 + HALF], in_=acc_r[:], func=FUNC.Square)
+            nc.scalar.activation(out=a_t[:, c0 : c0 + HALF], in_=banks[s][0][:], func=FUNC.Square)
             if s in ACT_I:
-                nc.scalar.activation(out=b_t[:, c0 : c0 + HALF], in_=acc_i[:], func=FUNC.Square)
+                nc.scalar.activation(out=b_t[:, c0 : c0 + HALF], in_=banks[s][1][:], func=FUNC.Square)
+
+        def squares_vector(s):
+            pk, c0 = place(s)
+            if s not in ACT_I:
+                nc.vector.tensor_reduce(
+                    out=sq[pk][1][:, c0 : c0 + HALF],
+                    in_=banks[s][1][:].unsqueeze(2).to_broadcast([P, HALF, 2]),
+                    axis=AXIS.X,
+                    op=ALU.mult,
+                )
+
+        def adds(s):
+            pk, c0 = place(s)
+            a_t, b_t = sq[pk]
+            ready[pk].append(c0)
+            per = UNITS_PER_ADD.get(pk, 4)
+            done = sorted(ready[pk])
+            if per == 1:
+                first = c0
+            elif per == 2:
+                first = N * (c0 // N)
+                if first not in done or first + HALF not in done:
+                    return
             else:
-                nc.vector.tensor_tensor(out=b_t[:, c0 : c0 + HALF], in0=acc_i[:], in1=copies[s][:], op=ALU.mult)
-            count[pk][tt] += 1
-            if pk in VU_PAIRS:
-                cols = slice(c0, c0 + HALF)
-                nc.vector.tensor_tensor(out=a_t[:, cols], in0=a_t[:, cols], in1=b_t[:, cols], op=ALU.add)
-                pending.append((s + LAG_V, pk, c0, HALF))
-            elif pk in V1_PAIRS:
-                if count[pk][tt] == 2:
-                    cols = slice(N * tt, N * (tt + 1))
-                    nc.vector.tensor_tensor(out=a_t[:, cols], in0=a_t[:, cols], in1=b_t[:, cols], op=ALU.add)
-                    pending.append((s + LAG_V, pk, N * tt, N))
-            elif pk in G1_PAIRS:
-                if count[pk][tt] == 2:
-                    cols = slice(N * tt, N * (tt + 1))
-                    nc.gpsimd.tensor_tensor(out=a_t[:, cols], in0=a_t[:, cols], in1=b_t[:, cols], op=ALU.add)
-                    pending.append((s + LAG_G1, pk, N * tt, N))
-            elif count[pk][0] + count[pk][1] == 4:
-                nc.gpsimd.tensor_tensor(out=a_t[:], in0=a_t[:], in1=b_t[:], op=ALU.add)
-                pending.append((s + LAG_G2, pk, 0, N))
-                pending.append((s + LAG_G2 + 2, pk, N, N))
+                first = 0
+                if len(done) < 4:
+                    return
+            width = per * HALF
+            cols = slice(first, first + width)
+            nc.gpsimd.tensor_tensor(out=a_t[:, cols], in0=a_t[:, cols], in1=b_t[:, cols], op=ALU.add)
+            for k in range(0, width, N):
+                pending.append((s + LAG[per] + k // HALF, pk, first + k, min(N, width - k)))
 
         def finish(pk, c0, width):
-            a_t, b_t = sq[pk]
-            part = b_t[:, c0 : c0 + width]
-            nc.scalar.activation(out=part, in_=a_t[:, c0 : c0 + width], func=FUNC.Ln)
+            a_t = sq[pk][0]
+            part = a_t[:, c0 : c0 + width]
+            nc.scalar.activation(out=part, in_=part, func=FUNC.Ln)
             g = pk // 2
             t = 2 * (pk % 2) + c0 // N
             n0 = c0 % N
@@ -214,28 +222,26 @@ def tile_dft_t_kernel(tc, x, dft_real, dft_imag, out):
         quantise("w10")
         mm(0)
         mm(1)
-        copy_i(0)
-        copy_i(1)
         for s in range(n_units):
             if s == 1:
                 transposes("w11", ("tp", "tp"))
             if s == 2:
                 quantise("w11")
-            g = s // 8 + 1
-            if g < GROUPS and s % 8 == X_T:
-                transposes("x%d" % g, ("tp", "tp"))
-            if g < GROUPS and s % 8 == X_Q:
-                quantise("x%d" % g)
+            if s in at_t:
+                transposes("x%d" % at_t[s], ("tp", "tp"))
             if s + 2 < n_units:
                 mm(s + 2)
-            squares(s)
-            copy_i(s + 2)
+            squares_scalar(s)
+            if s in at_x:
+                exits("x%d" % at_x[s], "vv")
+            if s in at_q:
+                quantise("x%d" % at_q[s])
+            squares_vector(s)
+            adds(s)
             if s == 0:
                 exits("w01", "av")
             if s == 1:
                 quantise("w01")
                 exits("w11", "av")
-            if g < GROUPS and s % 8 == X_X:
-                exits("x%d" % g, "vv")
             finish_due(s)
         finish_due(10 * n_units)

@@ -14,14 +14,17 @@ AXIS = mybir.AxisListType
 
 B, K, N = 4096, 512, 1024
 FLOPS = 2 * B * K * 2 * N
+
 P = 128
 HALF = 512
-GROUPS = 8
-ACT_I = (0, 1, 2, 4, 5, 11, 19, 27, 35, 39, 43, 51)
-LAG = {4: 6, 2: 4, 1: 4}
-X_T, X_X, X_Q = 0, 1, 3
-FIRST = (2, 3, 4)
-UNITS_PER_ADD = {0: 1, 1: 1, 14: 2, 15: 1}
+TILES = 4
+GROUPS = B // (TILES * P)
+UNITS_PER_GROUP = 2 * TILES
+UNITS = GROUPS * UNITS_PER_GROUP
+PAIRS = UNITS // 4
+AHEAD = 2
+UNIT_LAG = 4
+PAIR_LAG = 6
 
 
 def tile_dft_t_kernel(tc, x, dft_real, dft_imag, out):
@@ -31,217 +34,189 @@ def tile_dft_t_kernel(tc, x, dft_real, dft_imag, out):
         const = ctx.enter_context(tc.tile_pool(name="const", bufs=1))
         raw = ctx.enter_context(tc.tile_pool(name="raw", bufs=1))
         keep = ctx.enter_context(tc.tile_pool(name="keep", bufs=1))
-        stage = ctx.enter_context(tc.tile_pool(name="stage", bufs=3))
+        stage = ctx.enter_context(tc.tile_pool(name="stage", bufs=1))
         work = ctx.enter_context(tc.tile_pool(name="work", bufs=1))
         psum = ctx.enter_context(tc.psum_pool(name="psum", bufs=1))
 
-        raws = {}
+        raw_of = {}
+
+        def load(name, blocks):
+            loaded = raw.tile([P, TILES * K], BF16, name="raw_" + name)
+            nc.sync.dma_start(out=loaded[:].rearrange("p (b k) -> p b k", b=TILES), in_=blocks)
+            raw_of[name] = loaded
 
         def load_x(g):
-            t = raw.tile([P, 4 * K], BF16, name="rawx%d" % g)
-            nc.sync.dma_start(
-                out=t[:].rearrange("p (t k) -> p t k", t=4),
-                in_=x[512 * g : 512 * (g + 1), :].rearrange("(p t) k -> p t k", t=4),
-            )
-            raws["x%d" % g] = t
+            group_rows = x[TILES * P * g : TILES * P * (g + 1), :]
+            load("x%d" % g, group_rows.rearrange("(p b) k -> p b k", b=TILES))
 
-        def load_w(m, h):
-            src = (dft_real, dft_imag)[m]
-            t = raw.tile([P, 4 * K], BF16, name="raww%d%d" % (m, h))
-            nc.sync.dma_start(
-                out=t[:].rearrange("p (t k) -> p t k", t=4),
-                in_=src[HALF * h : HALF * (h + 1), :].rearrange("(t p) k -> p t k", p=P),
-            )
-            raws["w%d%d" % (m, h)] = t
+        def load_w(letter, matrix, h):
+            half_rows = matrix[HALF * h : HALF * (h + 1), :]
+            load(letter + "%d" % h, half_rows.rearrange("(b p) k -> p b k", p=P))
 
         load_x(0)
-        load_w(0, 0)
-        load_w(1, 0)
-        load_w(0, 1)
-        load_w(1, 1)
+        load_w("r", dft_real, 0)
+        load_w("i", dft_imag, 0)
+        load_w("r", dft_real, 1)
+        load_w("i", dft_imag, 1)
         for g in range(1, GROUPS):
             load_x(g)
 
-        ident = const.tile([P, P], F32, name="ident")
-        make_identity(nc, ident[:])
-        warm = const.tile([P, 1], F32, name="warm")
-        nc.vector.memset(warm[:], 1.0)
-        warm2 = const.tile([P, 1], F32, name="warm2")
-        nc.scalar.activation(out=warm2[:], in_=warm[:], func=FUNC.Ln)
+        identity = const.tile([P, P], F32, name="identity")
+        make_identity(nc, identity[:])
+        one = const.tile([P, 1], F32, name="one")
+        nc.vector.memset(one[:], 1.0)
+        zero = const.tile([P, 1], F32, name="zero")
+        nc.scalar.activation(out=zero[:], in_=one[:], func=FUNC.Ln)
 
-        tbanks = {}
+        transposed_of = {}
         grouped_of = {}
-        quantised = {}
+        quantised_of = {}
 
-        def transposes(name, tags):
-            words = raws[name][:].bitcast(F32)
-            pair = []
-            for half in range(2):
-                bank = psum.tile([P, 2, 2, P], F32, tag=tags[half], name="t%d%s" % (half, name),
-                                 bufs=(2 if tags[half] == "tp" else 3))
-                for bb in range(2):
+        def transpose(name):
+            raw_words = raw_of[name][:].bitcast(F32)
+            banks = []
+            for first_block in range(0, TILES, 2):
+                bank = psum.tile([P, 2, 2, P], F32, tag="t", name="t%d_%s" % (first_block, name), bufs=2)
+                for b in range(2):
                     for u in range(2):
-                        c0 = 256 * (2 * half + bb) + 128 * u
-                        nc.tensor.transpose(bank[:, bb, u, :], words[:, c0 : c0 + 128], ident[:])
-                pair.append(bank)
-            tbanks[name] = pair
+                        w0 = (K // 2) * (first_block + b) + P * u
+                        nc.tensor.transpose(bank[:, b, u, :], raw_words[:, w0 : w0 + P], identity[:])
+                banks.append(bank)
+            transposed_of[name] = banks
 
-        def exits(name, engines):
-            grouped = stage.tile([P, 4 * HALF], BF16, tag="grouped", name="g" + name, align_bytes=64)
-            gw = grouped[:].bitcast(F32).rearrange("p (b c u) -> p b c u", b=4, u=2)
-            for half in range(2):
-                src_view = tbanks[name][half][:].rearrange("p b u c -> p b c u")
-                dst_view = gw[:, 2 * half : 2 * half + 2]
-                if engines[half] == "a":
-                    nc.scalar.copy(out=dst_view, in_=src_view)
-                else:
-                    nc.vector.tensor_copy(out=dst_view, in_=src_view)
+        def copy_out(name, engines):
+            grouped = stage.tile([P, TILES * P * 4], BF16, tag="grouped", name="grouped_" + name, bufs=3,
+                                 align_bytes=64)
+            grouped_words = grouped[:].bitcast(F32).rearrange("p (b c u) -> p b c u", b=TILES, u=2)
+            for i, bank in enumerate(transposed_of[name]):
+                copy = nc.scalar.copy if engines[i] == "scalar" else nc.vector.tensor_copy
+                copy(out=grouped_words[:, 2 * i : 2 * i + 2], in_=bank[:].rearrange("p b u c -> p b c u"))
             grouped_of[name] = grouped
 
         def quantise(name):
-            codes = keep.tile([P, HALF], U32, name="c" + name, align_bytes=64)
-            scales = keep.tile([P, HALF], U8, name="s" + name, align_bytes=64)
+            codes = keep.tile([P, TILES * P], U32, name="codes_" + name, align_bytes=64)
+            scales = keep.tile([P, TILES * P], U8, name="scales_" + name, align_bytes=64)
             nc.vector.quantize_mx(out=codes[:].bitcast(FP8X4), scales=scales[:], in_=grouped_of[name][:])
-            quantised[name] = (codes, scales)
+            quantised_of[name] = (codes, scales)
 
-        units = [(0, t, 0) for t in range(4)] + [(0, t, 1) for t in range(4)]
-        for g in range(1, GROUPS):
-            units += [(g, t, h) for t in range(4) for h in range(2)]
-        n_units = len(units)
+        def place(s):
+            g, j = divmod(s, UNITS_PER_GROUP)
+            if g == 0:
+                return g, j % TILES, j // TILES
+            return g, j // 2, j % 2
 
-        at_t = {}
-        at_x = {}
-        at_q = {}
-        for g in range(1, GROUPS):
-            base = 8 * (g - 1)
-            steps = FIRST if g == 1 else (base + X_T, base + X_X, base + X_Q)
-            at_t[steps[0]] = g
-            at_x[steps[1]] = g
-            at_q[steps[2]] = g
+        def columns(s):
+            g, t, h = place(s)
+            return 2 * g + t // 2, N * (t % 2) + HALF * h
 
-        banks = {}
+        def by_unit(pair):
+            return pair < 2 or pair >= PAIRS - 2
 
-        def mm(s):
-            g, t, h = units[s]
-            xc, xs = quantised["x%d" % g]
-            pair = []
-            for m in range(2):
-                wc, ws = quantised["w%d%d" % (m, h)]
-                acc = psum.tile([P, HALF], F32, tag=("r", "i")[m], name="acc%d_%d" % (m, s), bufs=3)
+        def next_group(s):
+            g = s // UNITS_PER_GROUP + 1
+            return "x%d" % g if g < GROUPS else None
+
+        def scalar_squares_both(s):
+            return s < 4 or (s % UNITS_PER_GROUP == 3 and next_group(s) is not None)
+
+        products_of = {}
+        squares_of = {}
+
+        def matmuls(s):
+            g, t, h = place(s)
+            x_codes, x_scales = quantised_of["x%d" % g]
+            tile_rows = slice(P * t, P * (t + 1))
+            products = []
+            for letter in ("r", "i"):
+                w_codes, w_scales = quantised_of[letter + "%d" % h]
+                bank = psum.tile([P, HALF], F32, tag=letter, name="%s_%d" % (letter, s), bufs=AHEAD + 1)
                 nc.tensor.matmul_mx(
-                    out=acc[:],
-                    lhsT=xc[:, P * t : P * (t + 1)].bitcast(FP8X4),
-                    lhsT_scale=xs[:, P * t : P * (t + 1)],
-                    rhs=wc[:].bitcast(FP8X4),
-                    rhs_scale=ws[:],
+                    out=bank[:],
+                    lhsT=x_codes[:, tile_rows].bitcast(FP8X4),
+                    lhsT_scale=x_scales[:, tile_rows],
+                    rhs=w_codes[:].bitcast(FP8X4),
+                    rhs_scale=w_scales[:],
                     start=True,
                     stop=True,
                 )
-                pair.append(acc)
-            banks[s] = pair
+                products.append(bank)
+            products_of[s] = products
 
-        sq = {}
-        ready = {}
-        pending = []
-        served = [0]
+        def squares_on_scalar(s):
+            pair, c0 = columns(s)
+            if pair not in squares_of:
+                real = work.tile([P, 2 * N], F32, tag="real", name="real_%d" % pair, bufs=6)
+                imag = work.tile([P, 2 * N], F32, tag="imag", name="imag_%d" % pair, bufs=4)
+                squares_of[pair] = (real, imag)
+            real, imag = squares_of[pair]
+            nc.scalar.activation(out=real[:, c0 : c0 + HALF], in_=products_of[s][0][:], func=FUNC.Square)
+            if scalar_squares_both(s):
+                nc.scalar.activation(out=imag[:, c0 : c0 + HALF], in_=products_of[s][1][:], func=FUNC.Square)
 
-        def place(s):
-            g, t, h = units[s]
-            return 2 * g + t // 2, N * (t % 2) + HALF * h
+        def squares_on_vector(s):
+            if scalar_squares_both(s):
+                return
+            pair, c0 = columns(s)
+            nc.vector.tensor_reduce(
+                out=squares_of[pair][1][:, c0 : c0 + HALF],
+                in_=products_of[s][1][:].unsqueeze(2).to_broadcast([P, HALF, 2]),
+                axis=AXIS.X,
+                op=ALU.mult,
+            )
 
-        def squares_scalar(s):
-            pk, c0 = place(s)
-            if pk not in sq:
-                a_t = work.tile([P, 2 * N], F32, tag="a", name="a%d" % pk, bufs=6)
-                b_t = work.tile([P, 2 * N], F32, tag="b", name="b%d" % pk, bufs=4)
-                sq[pk] = (a_t, b_t)
-                ready[pk] = []
-            a_t, b_t = sq[pk]
-            nc.scalar.activation(out=a_t[:, c0 : c0 + HALF], in_=banks[s][0][:], func=FUNC.Square)
-            if s in ACT_I:
-                nc.scalar.activation(out=b_t[:, c0 : c0 + HALF], in_=banks[s][1][:], func=FUNC.Square)
+        def add(pair, c0, width):
+            real, imag = squares_of[pair]
+            cols = slice(c0, c0 + width)
+            nc.gpsimd.tensor_tensor(out=real[:, cols], in0=real[:, cols], in1=imag[:, cols], op=ALU.add)
 
-        def squares_vector(s):
-            pk, c0 = place(s)
-            if s not in ACT_I:
-                nc.vector.tensor_reduce(
-                    out=sq[pk][1][:, c0 : c0 + HALF],
-                    in_=banks[s][1][:].unsqueeze(2).to_broadcast([P, HALF, 2]),
-                    axis=AXIS.X,
-                    op=ALU.mult,
-                )
+        def log_and_store(pair, c0, width):
+            sums = squares_of[pair][0][:, c0 : c0 + width]
+            nc.scalar.activation(out=sums, in_=sums, func=FUNC.Ln)
+            g, t = pair // 2, 2 * (pair % 2) + c0 // N
+            group_rows = out[TILES * P * g : TILES * P * (g + 1), :].rearrange("(p t) n -> p t n", t=TILES)
+            nc.sync.dma_start(out=group_rows[:, t, c0 % N : c0 % N + width], in_=sums)
 
-        def adds(s):
-            pk, c0 = place(s)
-            a_t, b_t = sq[pk]
-            ready[pk].append(c0)
-            per = UNITS_PER_ADD.get(pk, 4)
-            done = sorted(ready[pk])
-            if per == 1:
-                first = c0
-            elif per == 2:
-                first = N * (c0 // N)
-                if first not in done or first + HALF not in done:
-                    return
-            else:
-                first = 0
-                if len(done) < 4:
-                    return
-            width = per * HALF
-            cols = slice(first, first + width)
-            nc.gpsimd.tensor_tensor(out=a_t[:, cols], in0=a_t[:, cols], in1=b_t[:, cols], op=ALU.add)
-            for k in range(0, width, N):
-                pending.append((s + LAG[per] + k // HALF, pk, first + k, min(N, width - k)))
-
-        def finish(pk, c0, width):
-            a_t = sq[pk][0]
-            part = a_t[:, c0 : c0 + width]
-            nc.scalar.activation(out=part, in_=part, func=FUNC.Ln)
-            g = pk // 2
-            t = 2 * (pk % 2) + c0 // N
-            n0 = c0 % N
-            dst = out[512 * g : 512 * (g + 1), :].rearrange("(p t) n -> p t n", t=4)
-            nc.sync.dma_start(out=dst[:, t, n0 : n0 + width], in_=part)
-
-        def finish_due(s):
-            pending[served[0] :] = sorted(pending[served[0] :])
-            while served[0] < len(pending) and pending[served[0]][0] <= s:
-                item = pending[served[0]]
-                served[0] += 1
-                finish(item[1], item[2], item[3])
-
-        transposes("x0", ("tp", "tp"))
-        transposes("w00", ("i", "i"))
-        exits("x0", "va")
-        transposes("w10", ("tp", "tp"))
+        transpose("x0")
+        transpose("r0")
+        copy_out("x0", ("vector", "scalar"))
+        transpose("i0")
         quantise("x0")
-        exits("w00", "av")
-        quantise("w00")
-        transposes("w01", ("i", "r"))
-        exits("w10", "av")
-        quantise("w10")
-        mm(0)
-        mm(1)
-        for s in range(n_units):
-            if s == 1:
-                transposes("w11", ("tp", "tp"))
-            if s == 2:
-                quantise("w11")
-            if s in at_t:
-                transposes("x%d" % at_t[s], ("tp", "tp"))
-            if s + 2 < n_units:
-                mm(s + 2)
-            squares_scalar(s)
-            if s in at_x:
-                exits("x%d" % at_x[s], "vv")
-            if s in at_q:
-                quantise("x%d" % at_q[s])
-            squares_vector(s)
-            adds(s)
-            if s == 0:
-                exits("w01", "av")
-            if s == 1:
-                quantise("w01")
-                exits("w11", "av")
-            finish_due(s)
-        finish_due(10 * n_units)
+        copy_out("r0", ("scalar", "vector"))
+        quantise("r0")
+        transpose("r1")
+        copy_out("i0", ("scalar", "vector"))
+        quantise("i0")
+        for s in range(AHEAD):
+            matmuls(s)
+        copy_out("r1", ("vector", "vector"))
+        transpose("i1")
+        quantise("r1")
+        copy_out("i1", ("vector", "vector"))
+        quantise("i1")
+
+        for s in range(UNITS + max(UNIT_LAG, PAIR_LAG - 2)):
+            j = s % UNITS_PER_GROUP
+            if next_group(s) and j == 0:
+                transpose(next_group(s))
+            if s + AHEAD < UNITS:
+                matmuls(s + AHEAD)
+            if s < UNITS:
+                squares_on_scalar(s)
+                if next_group(s) and j == 1:
+                    copy_out(next_group(s), ("vector", "vector"))
+                if next_group(s) and j == 3:
+                    quantise(next_group(s))
+                squares_on_vector(s)
+                pair, c0 = columns(s)
+                if by_unit(pair):
+                    add(pair, c0, HALF)
+                elif s % 4 == 3:
+                    add(pair, 0, 2 * N)
+            if 0 <= s - UNIT_LAG < UNITS:
+                pair, c0 = columns(s - UNIT_LAG)
+                if by_unit(pair):
+                    log_and_store(pair, c0, HALF)
+            for row_tile in range(2):
+                pair, rest = divmod(s - PAIR_LAG - 2 * row_tile - 3, 4)
+                if rest == 0 and 0 <= pair < PAIRS and not by_unit(pair):
+                    log_and_store(pair, N * row_tile, N)

from contextlib import ExitStack

import concourse.mybir as mybir
from concourse.masks import make_identity

F32 = mybir.dt.float32
BF16 = mybir.dt.bfloat16
U32 = mybir.dt.uint32
U8 = mybir.dt.uint8
FP8X4 = mybir.dt.float8_e4m3fn_x4
FUNC = mybir.ActivationFunctionType
ALU = mybir.AluOpType
AXIS = mybir.AxisListType

B, K, N = 4096, 512, 1024
FLOPS = 2 * B * K * 2 * N

P = 128
HALF = 512
TILES = 4
GROUPS = B // (TILES * P)
UNITS_PER_GROUP = 2 * TILES
UNITS = GROUPS * UNITS_PER_GROUP
PAIRS = UNITS // 4
AHEAD = 2
UNIT_LAG = 4
PAIR_LAG = 6


def tile_dft_t_kernel(tc, x, dft_real, dft_imag, out):
    nc = tc.nc
    with ExitStack() as ctx:
        ctx.enter_context(tc.manual_schedule())
        const = ctx.enter_context(tc.tile_pool(name="const", bufs=1))
        raw = ctx.enter_context(tc.tile_pool(name="raw", bufs=1))
        keep = ctx.enter_context(tc.tile_pool(name="keep", bufs=1))
        stage = ctx.enter_context(tc.tile_pool(name="stage", bufs=1))
        work = ctx.enter_context(tc.tile_pool(name="work", bufs=1))
        psum = ctx.enter_context(tc.psum_pool(name="psum", bufs=1))

        raw_of = {}

        def load(name, blocks):
            loaded = raw.tile([P, TILES * K], BF16, name="raw_" + name)
            nc.sync.dma_start(out=loaded[:].rearrange("p (b k) -> p b k", b=TILES), in_=blocks)
            raw_of[name] = loaded

        def load_x(g):
            group_rows = x[TILES * P * g : TILES * P * (g + 1), :]
            load("x%d" % g, group_rows.rearrange("(p b) k -> p b k", b=TILES))

        def load_w(letter, matrix, h):
            half_rows = matrix[HALF * h : HALF * (h + 1), :]
            load(letter + "%d" % h, half_rows.rearrange("(b p) k -> p b k", p=P))

        load_x(0)
        load_w("r", dft_real, 0)
        load_w("i", dft_imag, 0)
        load_w("r", dft_real, 1)
        load_w("i", dft_imag, 1)
        for g in range(1, GROUPS):
            load_x(g)

        identity = const.tile([P, P], F32, name="identity")
        make_identity(nc, identity[:])
        one = const.tile([P, 1], F32, name="one")
        nc.vector.memset(one[:], 1.0)
        zero = const.tile([P, 1], F32, name="zero")
        nc.scalar.activation(out=zero[:], in_=one[:], func=FUNC.Ln)

        transposed_of = {}
        grouped_of = {}
        quantised_of = {}

        def transpose(name):
            raw_words = raw_of[name][:].bitcast(F32)
            banks = []
            for first_block in range(0, TILES, 2):
                bank = psum.tile([P, 2, 2, P], F32, tag="t", name="t%d_%s" % (first_block, name), bufs=2)
                for b in range(2):
                    for u in range(2):
                        w0 = (K // 2) * (first_block + b) + P * u
                        nc.tensor.transpose(bank[:, b, u, :], raw_words[:, w0 : w0 + P], identity[:])
                banks.append(bank)
            transposed_of[name] = banks

        def copy_out(name, engines):
            grouped = stage.tile([P, TILES * P * 4], BF16, tag="grouped", name="grouped_" + name, bufs=3,
                                 align_bytes=64)
            grouped_words = grouped[:].bitcast(F32).rearrange("p (b c u) -> p b c u", b=TILES, u=2)
            for i, bank in enumerate(transposed_of[name]):
                copy = nc.scalar.copy if engines[i] == "scalar" else nc.vector.tensor_copy
                copy(out=grouped_words[:, 2 * i : 2 * i + 2], in_=bank[:].rearrange("p b u c -> p b c u"))
            grouped_of[name] = grouped

        def quantise(name):
            codes = keep.tile([P, TILES * P], U32, name="codes_" + name, align_bytes=64)
            scales = keep.tile([P, TILES * P], U8, name="scales_" + name, align_bytes=64)
            nc.vector.quantize_mx(out=codes[:].bitcast(FP8X4), scales=scales[:], in_=grouped_of[name][:])
            quantised_of[name] = (codes, scales)

        def place(s):
            g, j = divmod(s, UNITS_PER_GROUP)
            if g == 0:
                return g, j % TILES, j // TILES
            return g, j // 2, j % 2

        def columns(s):
            g, t, h = place(s)
            return 2 * g + t // 2, N * (t % 2) + HALF * h

        def by_unit(pair):
            return pair < 2 or pair >= PAIRS - 2

        def next_group(s):
            g = s // UNITS_PER_GROUP + 1
            return "x%d" % g if g < GROUPS else None

        def scalar_squares_both(s):
            return s < 4 or (s % UNITS_PER_GROUP == 3 and next_group(s) is not None)

        products_of = {}
        squares_of = {}

        def matmuls(s):
            g, t, h = place(s)
            x_codes, x_scales = quantised_of["x%d" % g]
            tile_rows = slice(P * t, P * (t + 1))
            products = []
            for letter in ("r", "i"):
                w_codes, w_scales = quantised_of[letter + "%d" % h]
                bank = psum.tile([P, HALF], F32, tag=letter, name="%s_%d" % (letter, s), bufs=AHEAD + 1)
                nc.tensor.matmul_mx(
                    out=bank[:],
                    lhsT=x_codes[:, tile_rows].bitcast(FP8X4),
                    lhsT_scale=x_scales[:, tile_rows],
                    rhs=w_codes[:].bitcast(FP8X4),
                    rhs_scale=w_scales[:],
                    start=True,
                    stop=True,
                )
                products.append(bank)
            products_of[s] = products

        def squares_on_scalar(s):
            pair, c0 = columns(s)
            if pair not in squares_of:
                real = work.tile([P, 2 * N], F32, tag="real", name="real_%d" % pair, bufs=6)
                imag = work.tile([P, 2 * N], F32, tag="imag", name="imag_%d" % pair, bufs=4)
                squares_of[pair] = (real, imag)
            real, imag = squares_of[pair]
            nc.scalar.activation(out=real[:, c0 : c0 + HALF], in_=products_of[s][0][:], func=FUNC.Square)
            if scalar_squares_both(s):
                nc.scalar.activation(out=imag[:, c0 : c0 + HALF], in_=products_of[s][1][:], func=FUNC.Square)

        def squares_on_vector(s):
            if scalar_squares_both(s):
                return
            pair, c0 = columns(s)
            nc.vector.tensor_reduce(
                out=squares_of[pair][1][:, c0 : c0 + HALF],
                in_=products_of[s][1][:].unsqueeze(2).to_broadcast([P, HALF, 2]),
                axis=AXIS.X,
                op=ALU.mult,
            )

        def add(pair, c0, width):
            real, imag = squares_of[pair]
            cols = slice(c0, c0 + width)
            nc.gpsimd.tensor_tensor(out=real[:, cols], in0=real[:, cols], in1=imag[:, cols], op=ALU.add)

        def log_and_store(pair, c0, width):
            sums = squares_of[pair][0][:, c0 : c0 + width]
            nc.scalar.activation(out=sums, in_=sums, func=FUNC.Ln)
            g, t = pair // 2, 2 * (pair % 2) + c0 // N
            group_rows = out[TILES * P * g : TILES * P * (g + 1), :].rearrange("(p t) n -> p t n", t=TILES)
            nc.sync.dma_start(out=group_rows[:, t, c0 % N : c0 % N + width], in_=sums)

        transpose("x0")
        transpose("r0")
        copy_out("x0", ("vector", "scalar"))
        transpose("i0")
        quantise("x0")
        copy_out("r0", ("scalar", "vector"))
        quantise("r0")
        transpose("r1")
        copy_out("i0", ("scalar", "vector"))
        quantise("i0")
        for s in range(AHEAD):
            matmuls(s)
        copy_out("r1", ("vector", "vector"))
        transpose("i1")
        quantise("r1")
        copy_out("i1", ("vector", "vector"))
        quantise("i1")

        for s in range(UNITS + max(UNIT_LAG, PAIR_LAG - 2)):
            j = s % UNITS_PER_GROUP
            if next_group(s) and j == 0:
                transpose(next_group(s))
            if s + AHEAD < UNITS:
                matmuls(s + AHEAD)
            if s < UNITS:
                squares_on_scalar(s)
                if next_group(s) and j == 1:
                    copy_out(next_group(s), ("vector", "vector"))
                if next_group(s) and j == 3:
                    quantise(next_group(s))
                squares_on_vector(s)
                pair, c0 = columns(s)
                if by_unit(pair):
                    add(pair, c0, HALF)
                elif s % 4 == 3:
                    add(pair, 0, 2 * N)
            if 0 <= s - UNIT_LAG < UNITS:
                pair, c0 = columns(s - UNIT_LAG)
                if by_unit(pair):
                    log_and_store(pair, c0, HALF)
            for row_tile in range(2):
                pair, rest = divmod(s - PAIR_LAG - 2 * row_tile - 3, 4)
                if rest == 0 and 0 <= pair < PAIRS and not by_unit(pair):
                    log_and_store(pair, N * row_tile, N)
